import numpy as np
import ml_dtypes


def mxq(x, axis, fmt="e4m3"):
    dtype, down = {"e4m3": (ml_dtypes.float8_e4m3fn, 7), "e5m2": (ml_dtypes.float8_e5m2, 14)}[fmt]
    v = np.moveaxis(np.asarray(x, np.float32).astype(ml_dtypes.bfloat16).astype(np.float64), axis, -1)
    blocks = v.reshape(v.shape[:-1] + (-1, 32))
    amax = np.abs(blocks).max(-1, keepdims=True)
    byte = np.maximum(np.where(amax > 0, np.frexp(amax)[1] - 1 + 127, 0) - down, 1)
    scale = np.exp2(byte - 127.0)
    codes = (blocks / scale).astype(np.float32).astype(dtype).astype(np.float64)
    return np.moveaxis((codes * scale).reshape(v.shape), -1, axis)


WIDE = False


def mx_kscale(k):
    if not WIDE:
        return np.ones(k)
    levels = np.array([10, -10, 5, -5, 0])
    a = np.random.permutation(np.resize(levels, k // 512 * 4)).reshape(k // 512, 4)
    idx = np.arange(k)
    return np.exp2(a[idx // 512, idx % 128 // 32])


BF16 = ml_dtypes.bfloat16


def bf(x):
    return np.asarray(x, np.float32).astype(BF16)


def f64(x):
    return np.asarray(x).astype(np.float64)


B, D_IN, H1, H2, LAT, NQ, NL, NA = 2048, 4096, 2048, 1024, 512, 512, 2, 3


def circuit(th, P):
    ar, ai = np.cos(0.5 * th), np.zeros_like(th)
    br, bi = np.sin(0.5 * th), np.zeros_like(th)
    for l in range(NL):
        rx, ry, rz = P[l].T
        c, s = np.cos(0.5 * rx), np.sin(0.5 * rx)
        ar, ai, br, bi = c * ar + s * bi, c * ai - s * br, s * ai + c * br, c * bi - s * ar
        c, s = np.cos(0.5 * ry), np.sin(0.5 * ry)
        ar, ai, br, bi = c * ar - s * br, c * ai - s * bi, s * ar + c * br, s * ai + c * bi
        c, s = np.cos(0.5 * rz), np.sin(0.5 * rz)
        ar, ai, br, bi = c * ar + s * ai, c * ai - s * ar, c * br - s * bi, c * bi + s * br
    return (ar * ar + ai * ai) - (br * br + bi * bi)


def setup_inputs():
    s = mx_kscale(H2)
    return {"h_enc2": bf(np.maximum(np.random.standard_normal((B, H2)), 0.0) * s),
            "We3": bf(np.random.standard_normal((NQ, H2)) * 1.4 / np.sqrt(H2) / s),
            "be3": bf(np.random.standard_normal(NQ) * 0.3),
            "P": bf(np.random.standard_normal((NL, NQ, NA))),
            "Wd1": bf(np.random.standard_normal((H2, NQ)) * 1.7 / np.sqrt(NQ)),
            "bd1": bf(np.random.standard_normal(H2) * 0.3)}


def reference(h_enc2, We3, be3, P, Wd1, bd1):
    th = (mxq(f64(h_enc2), 1, "e4m3") @ mxq(f64(We3), 1, "e4m3").T) + f64(be3)
    z = circuit(th, f64(P))
    return np.maximum((mxq(z, 1, "e4m3") @ mxq(f64(Wd1), 1, "e4m3").T) + f64(bd1), 0.0)

@@ -1,0 +1,348 @@
+import math
+from contextlib import ExitStack
+
+import concourse.mybir as mybir
+from concourse.masks import make_identity
+
+F32 = mybir.dt.float32
+BF16 = mybir.dt.bfloat16
+U32 = mybir.dt.uint32
+U8 = mybir.dt.uint8
+FP8X4 = mybir.dt.float8_e4m3fn_x4
+ALU = mybir.AluOpType
+ACT = mybir.ActivationFunctionType
+
+P = 128
+PACK = 4
+K_PASS = P * PACK
+
+BATCH = 2048
+K1 = 1024
+QUBITS = 512
+N_OUT = 1024
+PASSES1 = K1 // K_PASS
+PAIRS = 2
+Q_TILES = QUBITS // P
+N_BANK = 512
+
+ROW_TILES = 2
+CHUNK = ROW_TILES * P
+N_CHUNKS = BATCH // CHUNK
+
+FLOPS = 2 * BATCH * K1 * QUBITS + 2 * BATCH * QUBITS * N_OUT
+
+TURN = 2.0 * math.pi
+ROUNDER = 12582912.0
+LARGEST_F32 = 3.4028234663852886e38
+TINY = 1e-30
+PHASE_STEPS = 3
+
+
+def tile_unifiedautoencodernet_pa_kernel(tc, h_enc2, We3, be3, P_angles, Wd1, bd1, out):
+    nc = tc.nc
+    with ExitStack() as ctx:
+        keep = ctx.enter_context(tc.tile_pool(name="keep", bufs=1))
+        small = ctx.enter_context(tc.tile_pool(name="small", bufs=1))
+        stage = ctx.enter_context(tc.tile_pool(name="stage", bufs=3))
+        results = ctx.enter_context(tc.tile_pool(name="results", bufs=4))
+        psum_turned = ctx.enter_context(tc.psum_pool(name="psum_turned", bufs=2))
+        psum_th = ctx.enter_context(tc.psum_pool(name="psum_th", bufs=4))
+        psum_out = ctx.enter_context(tc.psum_pool(name="psum_out", bufs=2))
+
+        angles_bf = small.tile([P, 2, PACK, 3], BF16)
+        nc.scalar.dma_start(out=angles_bf[:], in_=P_angles.rearrange("l (p t) a -> p l t a", t=PACK))
+        be3_bf = small.tile([P, PACK], BF16)
+        nc.scalar.dma_start(out=be3_bf[:], in_=be3.rearrange("(p t) -> p t", t=PACK))
+
+        h_raw = keep.tile([P, N_CHUNKS, ROW_TILES, K1], BF16)
+        w1_raw = keep.tile([P, Q_TILES, K1], BF16)
+        w2_raw = keep.tile([P, N_OUT // P, QUBITS], BF16)
+        bias = keep.tile([P, N_OUT], BF16)
+
+        def load_chunk(c):
+            rows = h_enc2[c * CHUNK : (c + 1) * CHUNK, :]
+            nc.sync.dma_start(out=h_raw[:, c], in_=rows.rearrange("(p i) k -> p i k", i=ROW_TILES))
+
+        load_chunk(0)
+        nc.sync.dma_start(out=w1_raw[:], in_=We3.rearrange("(p t) k -> p t k", t=Q_TILES))
+        load_chunk(1)
+        nc.sync.dma_start(out=w2_raw[:], in_=Wd1.rearrange("(i p) q -> p i q", p=P))
+        for c in range(2, N_CHUNKS):
+            load_chunk(c)
+        nc.sync.dma_start(out=bias[:], in_=bd1.partition_broadcast(P))
+
+        identity = keep.tile([P, P], F32)
+        make_identity(nc, identity[:])
+        rounder = small.tile([P, 1], F32)
+        nc.vector.memset(rounder[:], ROUNDER)
+        minus_half = small.tile([P, PACK], F32)
+        nc.vector.memset(minus_half[:], -0.5)
+        warm = small.tile([P, 1], F32)
+        nc.vector.memset(warm[:], 0.0)
+        nc.scalar.activation(out=warm[:], in_=warm[:], func=ACT.Sin)
+
+        def product(dst, a, b):
+            nc.vector.tensor_tensor(out=dst, in0=a, in1=b, op=ALU.mult)
+
+        def both(x):
+            return x.unsqueeze(1).to_broadcast([P, 2, PACK])
+
+        turns = small.tile([P, 2, 2, PACK, 3], F32)
+        nc.vector.tensor_scalar(
+            out=turns[:, 0], in0=angles_bf[:], scalar1=1.0 / TURN, scalar2=None, op0=ALU.mult
+        )
+        nc.vector.tensor_scalar(
+            out=turns[:, 1], in0=angles_bf[:], scalar1=1.0 / TURN, scalar2=0.25,
+            op0=ALU.mult, op1=ALU.add,
+        )
+        flat = "p f l t a -> p (f l t a)"
+        whole = small.tile([P, 2, 2, PACK, 3], F32)
+        nc.vector.tensor_scalar(
+            out=whole[:].rearrange(flat), in0=turns[:].rearrange(flat),
+            scalar1=ROUNDER, scalar2=ROUNDER, op0=ALU.add, op1=ALU.subtract,
+        )
+        nc.vector.tensor_tensor(
+            out=turns[:].rearrange(flat), in0=turns[:].rearrange(flat),
+            in1=whole[:].rearrange(flat), op=ALU.subtract,
+        )
+        trig = small.tile([P, 2, 2, PACK, 3], F32)
+        nc.scalar.activation(
+            out=trig[:].rearrange(flat), in_=turns[:].rearrange(flat), func=ACT.Sin, scale=TURN
+        )
+
+        def sin_of(layer, gate):
+            return trig[:, 0, layer, :, gate]
+
+        def cos_of(layer, gate):
+            return trig[:, 1, layer, :, gate]
+
+        def sin_cos_of(layer, gate):
+            return trig[:, :, layer, :, gate]
+
+        RX, RY, RZ = 0, 1, 2
+        SIN, COS = 0, 1
+        yz = small.tile([P, 2, PACK], F32)
+        product(yz[:], both(cos_of(1, RY)), sin_cos_of(1, RX))
+        x_parts = small.tile([P, 2, PACK], F32)
+        product(x_parts[:], both(sin_of(1, RY)), sin_cos_of(0, RZ))
+        y_parts = small.tile([P, 2, PACK], F32)
+        product(y_parts[:], both(yz[:, 0, :]), sin_cos_of(0, RZ))
+        wx = small.tile([P, PACK], F32)
+        nc.vector.tensor_tensor(out=wx[:], in0=y_parts[:, SIN, :], in1=x_parts[:, COS, :], op=ALU.subtract)
+        wy = small.tile([P, PACK], F32)
+        nc.vector.tensor_tensor(out=wy[:], in0=x_parts[:, SIN, :], in1=y_parts[:, COS, :], op=ALU.add)
+        z_parts = small.tile([P, 2, PACK], F32)
+        product(z_parts[:], both(yz[:, 1, :]), sin_cos_of(0, RY))
+        x_parts2 = small.tile([P, 2, PACK], F32)
+        product(x_parts2[:], both(wx[:]), sin_cos_of(0, RY))
+        a_c = small.tile([P, 2, PACK], F32)
+        nc.vector.tensor_tensor(
+            out=a_c[:, 0, :], in0=x_parts2[:, COS, :], in1=z_parts[:, SIN, :], op=ALU.subtract
+        )
+        wz = small.tile([P, PACK], F32)
+        nc.vector.tensor_tensor(out=wz[:], in0=x_parts2[:, SIN, :], in1=z_parts[:, COS, :], op=ALU.add)
+        wy_sin = small.tile([P, PACK], F32)
+        product(wy_sin[:], wy[:], sin_of(0, RX))
+        wz_cos = small.tile([P, PACK], F32)
+        product(wz_cos[:], wz[:], cos_of(0, RX))
+        nc.vector.tensor_tensor(out=a_c[:, 1, :], in0=wz_cos[:], in1=wy_sin[:], op=ALU.subtract)
+
+        squares = small.tile([P, 2, PACK], F32)
+        product(squares[:], a_c[:], a_c[:])
+        length2 = small.tile([P, PACK], F32)
+        nc.vector.scalar_tensor_tensor(
+            out=length2[:], in0=squares[:, 0, :], scalar=TINY, in1=squares[:, 1, :],
+            op0=ALU.add, op1=ALU.add,
+        )
+        inv_length = small.tile([P, PACK], F32)
+        nc.gpsimd.tensor_tensor(out=inv_length[:], in0=length2[:], in1=minus_half[:], op=ALU.pow)
+        twice_positive = small.tile([P, PACK], F32)
+        nc.vector.tensor_scalar(
+            out=twice_positive[:], in0=a_c[:, 0, :], scalar1=0.0, scalar2=2.0,
+            op0=ALU.is_ge, op1=ALU.mult,
+        )
+        inv_m = small.tile([P, PACK], F32)
+        nc.vector.scalar_tensor_tensor(
+            out=inv_m[:], in0=twice_positive[:], scalar=1.0, in1=inv_length[:],
+            op0=ALU.subtract, op1=ALU.mult,
+        )
+        amplitude = small.tile([P, PACK], F32)
+        product(amplitude[:], length2[:], inv_m[:])
+        unit = small.tile([P, 2, PACK], F32)
+        product(unit[:], a_c[:], both(inv_m[:]))
+        cos_goal = unit[:, 0, :]
+        sin_goal = unit[:, 1, :]
+
+        phase = small.tile([P, PACK], F32)
+        nc.vector.tensor_copy(out=phase[:], in_=sin_goal)
+        for step in range(PHASE_STEPS):
+            sin_x = small.tile([P, PACK], F32)
+            nc.scalar.activation(out=sin_x[:], in_=phase[:], func=ACT.Sin)
+            sin_half = small.tile([P, PACK], F32)
+            nc.scalar.activation(out=sin_half[:], in_=phase[:], func=ACT.Sin, scale=0.5)
+            base = small.tile([P, PACK], F32)
+            nc.vector.tensor_tensor(out=base[:], in0=phase[:], in1=sin_goal, op=ALU.add)
+            drop = small.tile([P, PACK], F32)
+            product(drop[:], cos_goal, sin_x[:])
+            half2 = small.tile([P, PACK], F32)
+            product(half2[:], sin_half[:], sin_half[:])
+            nc.vector.tensor_tensor(out=base[:], in0=base[:], in1=drop[:], op=ALU.subtract)
+            nc.vector.scalar_tensor_tensor(
+                out=half2[:], in0=half2[:], scalar=2.0, in1=sin_goal, op0=ALU.mult, op1=ALU.mult
+            )
+            nc.vector.tensor_tensor(out=phase[:], in0=base[:], in1=half2[:], op=ALU.subtract)
+
+        be3_turns = small.tile([P, PACK], F32)
+        nc.vector.tensor_scalar(
+            out=be3_turns[:], in0=be3_bf[:], scalar1=1.0 / TURN, scalar2=None, op0=ALU.mult
+        )
+        shift = small.tile([P, PACK], F32)
+        nc.vector.scalar_tensor_tensor(
+            out=shift[:], in0=phase[:], scalar=1.0 / TURN, in1=be3_turns[:],
+            op0=ALU.mult, op1=ALU.add,
+        )
+
+        h_codes = keep.tile([P, N_CHUNKS, PASSES1, CHUNK], U32, align_bytes=64)
+        h_scales = keep.tile([P, N_CHUNKS, PASSES1, CHUNK], U8, align_bytes=64)
+        w1_codes = keep.tile([P, Q_TILES, PASSES1, P], U32, align_bytes=64)
+        w1_scales = keep.tile([P, Q_TILES, PASSES1, P], U8, align_bytes=64)
+
+        def quantise_along_k1(row_tiles, codes, scales):
+            n_rows = len(row_tiles) * P
+            grouped = stage.tile([P, PASSES1, n_rows, PACK], BF16, align_bytes=64)
+            grouped_words = grouped[:].bitcast(F32)
+            for i, rows in enumerate(row_tiles):
+                words = rows.bitcast(F32)
+                turned = psum_turned.tile([P, PASSES1, PAIRS, P], F32)
+                for g in range(PASSES1):
+                    for u in range(PAIRS):
+                        first = (g * PAIRS + u) * P
+                        nc.tensor.transpose(turned[:, g, u, :], words[:, first : first + P], identity[:])
+                nc.scalar.copy(
+                    out=grouped_words[:, :, i * P : (i + 1) * P, :],
+                    in_=turned[:].rearrange("p g u r -> p g r u"),
+                )
+            nc.vector.quantize_mx(
+                out=codes.rearrange("p g r -> p (g r)").bitcast(FP8X4),
+                scales=scales.rearrange("p g r -> p (g r)"),
+                in_=grouped[:].rearrange("p g r j -> p (g r j)"),
+            )
+
+        def quantise_chunk(c):
+            quantise_along_k1([h_raw[:, c, i, :] for i in range(ROW_TILES)], h_codes[:, c], h_scales[:, c])
+
+        w2_codes = keep.tile([P, N_OUT], U32, align_bytes=64)
+        w2_scales = keep.tile([P, N_OUT], U8, align_bytes=64)
+
+        def quantise_w2():
+            words = w2_raw[:].bitcast(F32).rearrange("p i (w u) -> p i u w", u=PAIRS)
+            for pair in range(N_OUT // (2 * P)):
+                grouped2 = stage.tile([P, 2 * P, PACK], BF16, align_bytes=64)
+                turned = psum_turned.tile([P, 2, PAIRS, P], F32)
+                for i in range(2):
+                    for u in range(PAIRS):
+                        nc.tensor.transpose(turned[:, i, u, :], words[:, 2 * pair + i, u, :], identity[:])
+                nc.scalar.copy(
+                    out=grouped2[:].bitcast(F32).rearrange("p (i r) u -> p i r u", i=2),
+                    in_=turned[:].rearrange("p i u r -> p i r u"),
+                )
+                cols = slice(pair * 2 * P, (pair + 1) * 2 * P)
+                nc.vector.quantize_mx(
+                    out=w2_codes[:, cols].bitcast(FP8X4),
+                    scales=w2_scales[:, cols],
+                    in_=grouped2[:].rearrange("p r j -> p (r j)"),
+                )
+
+        def first_product(c):
+            banks = []
+            for b in range(Q_TILES // 2):
+                th_bank = psum_th.tile([P, 2, CHUNK], F32)
+                for i in range(2):
+                    t = 2 * b + i
+                    for g in range(PASSES1):
+                        nc.tensor.matmul_mx(
+                            out=th_bank[:, i, :],
+                            lhsT=w1_codes[:, t, g, :].bitcast(FP8X4),
+                            lhsT_scale=w1_scales[:, t, g, :],
+                            rhs=h_codes[:, c, g, :].bitcast(FP8X4),
+                            rhs_scale=h_scales[:, c, g, :],
+                            start=(g == 0),
+                            stop=(g == PASSES1 - 1),
+                        )
+                banks.append(th_bank)
+            return banks
+
+        def circuit(th_banks):
+            flat_tb = "p t b -> p (t b)"
+            angle = stage.tile([P, Q_TILES, CHUNK], F32)
+            for t in range(Q_TILES):
+                nc.scalar.activation(
+                    out=angle[:, t, :], in_=th_banks[t // 2][:, t % 2, :], func=ACT.Identity,
+                    scale=1.0 / TURN, bias=shift[:, t : t + 1],
+                )
+            nearest = stage.tile([P, Q_TILES, CHUNK], F32)
+            nc.scalar.activation(
+                out=nearest[:].rearrange(flat_tb), in_=angle[:].rearrange(flat_tb), func=ACT.Identity,
+                scale=1.0, bias=rounder[:],
+            )
+            nc.vector.scalar_tensor_tensor(
+                out=nearest[:].rearrange(flat_tb), in0=nearest[:].rearrange(flat_tb), scalar=ROUNDER,
+                in1=angle[:].rearrange(flat_tb), op0=ALU.subtract, op1=ALU.subtract,
+            )
+            sine = stage.tile([P, Q_TILES, CHUNK], F32)
+            nc.scalar.activation(
+                out=sine[:].rearrange(flat_tb), in_=nearest[:].rearrange(flat_tb), func=ACT.Sin, scale=-TURN
+            )
+            z_grouped = stage.tile([P, CHUNK, PACK], BF16, align_bytes=64)
+            nc.vector.tensor_tensor(
+                out=z_grouped[:],
+                in0=sine[:].rearrange("p t b -> p b t"),
+                in1=amplitude[:].unsqueeze(1).to_broadcast([P, CHUNK, PACK]),
+                op=ALU.mult,
+            )
+            z_codes = stage.tile([P, CHUNK], U32, align_bytes=64)
+            z_scales = stage.tile([P, CHUNK], U8, align_bytes=64)
+            nc.vector.quantize_mx(
+                out=z_codes[:].bitcast(FP8X4),
+                scales=z_scales[:],
+                in_=z_grouped[:].rearrange("p b t -> p (b t)"),
+            )
+            return z_codes, z_scales
+
+        def second_product(c, z_codes, z_scales):
+            result = results.tile([P, ROW_TILES, N_OUT], F32)
+            for i in range(ROW_TILES):
+                rows = slice(i * P, (i + 1) * P)
+                for n in range(N_OUT // N_BANK):
+                    cols = slice(n * N_BANK, (n + 1) * N_BANK)
+                    acc = psum_out.tile([P, N_BANK], F32)
+                    nc.tensor.matmul_mx(
+                        out=acc[:],
+                        lhsT=z_codes[:, rows].bitcast(FP8X4),
+                        lhsT_scale=z_scales[:, rows],
+                        rhs=w2_codes[:, cols].bitcast(FP8X4),
+                        rhs_scale=w2_scales[:, cols],
+                        start=True,
+                        stop=True,
+                    )
+                    nc.vector.tensor_tensor(out=result[:, i, cols], in0=acc[:], in1=bias[:, cols], op=ALU.add)
+                nc.gpsimd.tensor_scalar(
+                    out=result[:, i, :], in0=result[:, i, :], scalar1=LARGEST_F32, scalar2=0.0,
+                    op0=ALU.min, op1=ALU.max,
+                )
+            rows_out = out[c * CHUNK : (c + 1) * CHUNK, :]
+            nc.sync.dma_start(out=rows_out.rearrange("(p i) n -> p i n", i=ROW_TILES), in_=result[:])
+
+        quantise_chunk(0)
+        for t in range(Q_TILES):
+            quantise_along_k1([w1_raw[:, t, :]], w1_codes[:, t], w1_scales[:, t])
+        th_banks = first_product(0)
+        quantise_w2()
+        quantise_chunk(1)
+        for c in range(N_CHUNKS):
+            z_codes, z_scales = circuit(th_banks)
+            if c + 1 < N_CHUNKS:
+                th_banks = first_product(c + 1)
+            if c + 2 < N_CHUNKS:
+                quantise_chunk(c + 2)
+            second_product(c, z_codes, z_scales)

@@ -33,7 +33,6 @@ FLOPS = 2 * BATCH * K1 * QUBITS + 2 * BATCH * QUBITS * N_OUT
 
 TURN = 2.0 * math.pi
 ROUNDER = 12582912.0
-LARGEST_F32 = 3.4028234663852886e38
 TINY = 1e-30
 PHASE_STEPS = 3
 
@@ -44,7 +43,7 @@ def tile_unifiedautoencodernet_pa_kernel(tc, h_enc2, We3, be3, P_angles, Wd1, bd
         keep = ctx.enter_context(tc.tile_pool(name="keep", bufs=1))
         small = ctx.enter_context(tc.tile_pool(name="small", bufs=1))
         stage = ctx.enter_context(tc.tile_pool(name="stage", bufs=3))
-        results = ctx.enter_context(tc.tile_pool(name="results", bufs=4))
+        results = ctx.enter_context(tc.tile_pool(name="results", bufs=6))
         psum_turned = ctx.enter_context(tc.psum_pool(name="psum_turned", bufs=2))
         psum_th = ctx.enter_context(tc.psum_pool(name="psum_th", bufs=4))
         psum_out = ctx.enter_context(tc.psum_pool(name="psum_out", bufs=2))
@@ -73,8 +72,6 @@ def tile_unifiedautoencodernet_pa_kernel(tc, h_enc2, We3, be3, P_angles, Wd1, bd
 
         identity = keep.tile([P, P], F32)
         make_identity(nc, identity[:])
-        rounder = small.tile([P, 1], F32)
-        nc.vector.memset(rounder[:], ROUNDER)
         minus_half = small.tile([P, PACK], F32)
         nc.vector.memset(minus_half[:], -0.5)
         warm = small.tile([P, 1], F32)
@@ -281,9 +278,9 @@ def tile_unifiedautoencodernet_pa_kernel(tc, h_enc2, We3, be3, P_angles, Wd1, bd
                     scale=1.0 / TURN, bias=shift[:, t : t + 1],
                 )
             nearest = stage.tile([P, Q_TILES, CHUNK], F32)
-            nc.scalar.activation(
-                out=nearest[:].rearrange(flat_tb), in_=angle[:].rearrange(flat_tb), func=ACT.Identity,
-                scale=1.0, bias=rounder[:],
+            nc.gpsimd.tensor_scalar(
+                out=nearest[:].rearrange(flat_tb), in0=angle[:].rearrange(flat_tb),
+                scalar1=1.0, scalar2=ROUNDER, op0=ALU.mult, op1=ALU.add,
             )
             nc.vector.scalar_tensor_tensor(
                 out=nearest[:].rearrange(flat_tb), in0=nearest[:].rearrange(flat_tb), scalar=ROUNDER,
@@ -310,9 +307,10 @@ def tile_unifiedautoencodernet_pa_kernel(tc, h_enc2, We3, be3, P_angles, Wd1, bd
             return z_codes, z_scales
 
         def second_product(c, z_codes, z_scales):
-            result = results.tile([P, ROW_TILES, N_OUT], F32)
+            rows_out = out[c * CHUNK : (c + 1) * CHUNK, :].rearrange("(p i) n -> p i n", i=ROW_TILES)
             for i in range(ROW_TILES):
                 rows = slice(i * P, (i + 1) * P)
+                result = results.tile([P, N_OUT], F32)
                 for n in range(N_OUT // N_BANK):
                     cols = slice(n * N_BANK, (n + 1) * N_BANK)
                     acc = psum_out.tile([P, N_BANK], F32)
@@ -325,13 +323,9 @@ def tile_unifiedautoencodernet_pa_kernel(tc, h_enc2, We3, be3, P_angles, Wd1, bd
                         start=True,
                         stop=True,
                     )
-                    nc.vector.tensor_tensor(out=result[:, i, cols], in0=acc[:], in1=bias[:, cols], op=ALU.add)
-                nc.gpsimd.tensor_scalar(
-                    out=result[:, i, :], in0=result[:, i, :], scalar1=LARGEST_F32, scalar2=0.0,
-                    op0=ALU.min, op1=ALU.max,
-                )
-            rows_out = out[c * CHUNK : (c + 1) * CHUNK, :]
-            nc.sync.dma_start(out=rows_out.rearrange("(p i) n -> p i n", i=ROW_TILES), in_=result[:])
+                    nc.vector.tensor_tensor(out=result[:, cols], in0=acc[:], in1=bias[:, cols], op=ALU.add)
+                nc.scalar.activation(out=result[:], in_=result[:], func=ACT.Relu)
+                nc.sync.dma_start(out=rows_out[:, i, :], in_=result[:])
 
         quantise_chunk(0)
         for t in range(Q_TILES):

@@ -35,6 +35,7 @@ TURN = 2.0 * math.pi
 ROUNDER = 12582912.0
 TINY = 1e-30
 PHASE_STEPS = 3
+HEAD_CHUNKS = 3
 
 
 def tile_unifiedautoencodernet_pa_kernel(tc, h_enc2, We3, be3, P_angles, Wd1, bd1, out):
@@ -45,8 +46,8 @@ def tile_unifiedautoencodernet_pa_kernel(tc, h_enc2, We3, be3, P_angles, Wd1, bd
         stage = ctx.enter_context(tc.tile_pool(name="stage", bufs=3))
         results = ctx.enter_context(tc.tile_pool(name="results", bufs=6))
         psum_turned = ctx.enter_context(tc.psum_pool(name="psum_turned", bufs=2))
-        psum_th = ctx.enter_context(tc.psum_pool(name="psum_th", bufs=4))
-        psum_out = ctx.enter_context(tc.psum_pool(name="psum_out", bufs=2))
+        psum_th = ctx.enter_context(tc.psum_pool(name="psum_th", bufs=2))
+        psum_out = ctx.enter_context(tc.psum_pool(name="psum_out", bufs=4))
 
         angles_bf = small.tile([P, 2, PACK, 3], BF16)
         nc.scalar.dma_start(out=angles_bf[:], in_=P_angles.rearrange("l (p t) a -> p l t a", t=PACK))
@@ -204,29 +205,34 @@ def tile_unifiedautoencodernet_pa_kernel(tc, h_enc2, We3, be3, P_angles, Wd1, bd
         w1_codes = keep.tile([P, Q_TILES, PASSES1, P], U32, align_bytes=64)
         w1_scales = keep.tile([P, Q_TILES, PASSES1, P], U8, align_bytes=64)
 
-        def quantise_along_k1(row_tiles, codes, scales):
-            n_rows = len(row_tiles) * P
-            grouped = stage.tile([P, PASSES1, n_rows, PACK], BF16, align_bytes=64)
-            grouped_words = grouped[:].bitcast(F32)
-            for i, rows in enumerate(row_tiles):
+        def transpose_rows(row_tiles):
+            banks = []
+            for rows in row_tiles:
                 words = rows.bitcast(F32)
                 turned = psum_turned.tile([P, PASSES1, PAIRS, P], F32)
                 for g in range(PASSES1):
                     for u in range(PAIRS):
                         first = (g * PAIRS + u) * P
                         nc.tensor.transpose(turned[:, g, u, :], words[:, first : first + P], identity[:])
+                banks.append(turned)
+            return banks
+
+        def regroup_rows(banks):
+            grouped = stage.tile([P, PASSES1, len(banks) * P, PACK], BF16, align_bytes=64)
+            grouped_words = grouped[:].bitcast(F32)
+            for i, turned in enumerate(banks):
                 nc.scalar.copy(
                     out=grouped_words[:, :, i * P : (i + 1) * P, :],
                     in_=turned[:].rearrange("p g u r -> p g r u"),
                 )
+            return grouped
+
+        def quantise_rows(grouped, codes, scales):
             nc.vector.quantize_mx(
                 out=codes.rearrange("p g r -> p (g r)").bitcast(FP8X4),
                 scales=scales.rearrange("p g r -> p (g r)"),
                 in_=grouped[:].rearrange("p g r j -> p (g r j)"),
             )
-
-        def quantise_chunk(c):
-            quantise_along_k1([h_raw[:, c, i, :] for i in range(ROW_TILES)], h_codes[:, c], h_scales[:, c])
 
         w2_codes = keep.tile([P, N_OUT], U32, align_bytes=64)
         w2_scales = keep.tile([P, N_OUT], U8, align_bytes=64)
@@ -250,67 +256,107 @@ def tile_unifiedautoencodernet_pa_kernel(tc, h_enc2, We3, be3, P_angles, Wd1, bd
                     in_=grouped2[:].rearrange("p r j -> p (r j)"),
                 )
 
+        tiles = {}
+        flat_tb = "p t b -> p (t b)"
+
+        def exists(c):
+            return 0 <= c < N_CHUNKS
+
+        def transpose_chunk(c):
+            if exists(c):
+                tiles["turned", c] = transpose_rows([h_raw[:, c, i, :] for i in range(ROW_TILES)])
+
+        def regroup_chunk(c):
+            if exists(c):
+                tiles["grouped", c] = regroup_rows(tiles["turned", c])
+
+        def quantise_chunk(c):
+            if exists(c):
+                quantise_rows(tiles["grouped", c], h_codes[:, c], h_scales[:, c])
+
         def first_product(c):
-            banks = []
-            for b in range(Q_TILES // 2):
-                th_bank = psum_th.tile([P, 2, CHUNK], F32)
-                for i in range(2):
-                    t = 2 * b + i
-                    for g in range(PASSES1):
-                        nc.tensor.matmul_mx(
-                            out=th_bank[:, i, :],
-                            lhsT=w1_codes[:, t, g, :].bitcast(FP8X4),
-                            lhsT_scale=w1_scales[:, t, g, :],
-                            rhs=h_codes[:, c, g, :].bitcast(FP8X4),
-                            rhs_scale=h_scales[:, c, g, :],
-                            start=(g == 0),
-                            stop=(g == PASSES1 - 1),
-                        )
-                banks.append(th_bank)
-            return banks
+            if exists(c):
+                banks = []
+                for b in range(Q_TILES // 2):
+                    th_bank = psum_th.tile([P, 2, CHUNK], F32)
+                    for i in range(2):
+                        t = 2 * b + i
+                        for g in range(PASSES1):
+                            nc.tensor.matmul_mx(
+                                out=th_bank[:, i, :],
+                                lhsT=w1_codes[:, t, g, :].bitcast(FP8X4),
+                                lhsT_scale=w1_scales[:, t, g, :],
+                                rhs=h_codes[:, c, g, :].bitcast(FP8X4),
+                                rhs_scale=h_scales[:, c, g, :],
+                                start=(g == 0),
+                                stop=(g == PASSES1 - 1),
+                            )
+                    banks.append(th_bank)
+                tiles["th", c] = banks
 
-        def circuit(th_banks):
-            flat_tb = "p t b -> p (t b)"
-            angle = stage.tile([P, Q_TILES, CHUNK], F32)
-            for t in range(Q_TILES):
-                nc.scalar.activation(
-                    out=angle[:, t, :], in_=th_banks[t // 2][:, t % 2, :], func=ACT.Identity,
-                    scale=1.0 / TURN, bias=shift[:, t : t + 1],
+        def angle_in_turns(c):
+            if exists(c):
+                angle = stage.tile([P, Q_TILES, CHUNK], F32)
+                for t in range(Q_TILES):
+                    nc.scalar.activation(
+                        out=angle[:, t, :], in_=tiles["th", c][t // 2][:, t % 2, :], func=ACT.Identity,
+                        scale=1.0 / TURN, bias=shift[:, t : t + 1],
+                    )
+                tiles["angle", c] = angle
+
+        def nearest_turn(c):
+            if exists(c):
+                nearest = stage.tile([P, Q_TILES, CHUNK], F32)
+                nc.vector.tensor_scalar(
+                    out=nearest[:].rearrange(flat_tb), in0=tiles["angle", c][:].rearrange(flat_tb),
+                    scalar1=ROUNDER, scalar2=ROUNDER, op0=ALU.add, op1=ALU.subtract,
                 )
-            nearest = stage.tile([P, Q_TILES, CHUNK], F32)
-            nc.gpsimd.tensor_scalar(
-                out=nearest[:].rearrange(flat_tb), in0=angle[:].rearrange(flat_tb),
-                scalar1=1.0, scalar2=ROUNDER, op0=ALU.mult, op1=ALU.add,
-            )
-            nc.vector.scalar_tensor_tensor(
-                out=nearest[:].rearrange(flat_tb), in0=nearest[:].rearrange(flat_tb), scalar=ROUNDER,
-                in1=angle[:].rearrange(flat_tb), op0=ALU.subtract, op1=ALU.subtract,
-            )
-            sine = stage.tile([P, Q_TILES, CHUNK], F32)
-            nc.scalar.activation(
-                out=sine[:].rearrange(flat_tb), in_=nearest[:].rearrange(flat_tb), func=ACT.Sin, scale=-TURN
-            )
-            z_grouped = stage.tile([P, CHUNK, PACK], BF16, align_bytes=64)
-            nc.vector.tensor_tensor(
-                out=z_grouped[:],
-                in0=sine[:].rearrange("p t b -> p b t"),
-                in1=amplitude[:].unsqueeze(1).to_broadcast([P, CHUNK, PACK]),
-                op=ALU.mult,
-            )
-            z_codes = stage.tile([P, CHUNK], U32, align_bytes=64)
-            z_scales = stage.tile([P, CHUNK], U8, align_bytes=64)
-            nc.vector.quantize_mx(
-                out=z_codes[:].bitcast(FP8X4),
-                scales=z_scales[:],
-                in_=z_grouped[:].rearrange("p b t -> p (b t)"),
-            )
-            return z_codes, z_scales
+                tiles["nearest", c] = nearest
 
-        def second_product(c, z_codes, z_scales):
-            rows_out = out[c * CHUNK : (c + 1) * CHUNK, :].rearrange("(p i) n -> p i n", i=ROW_TILES)
-            for i in range(ROW_TILES):
+        def fraction_of_turn(c):
+            if exists(c):
+                angle = tiles["angle", c]
+                nc.vector.tensor_tensor(
+                    out=angle[:].rearrange(flat_tb), in0=angle[:].rearrange(flat_tb),
+                    in1=tiles["nearest", c][:].rearrange(flat_tb), op=ALU.subtract,
+                )
+
+        def sine_of_angle(c):
+            if exists(c):
+                sine = stage.tile([P, Q_TILES, CHUNK], F32)
+                nc.scalar.activation(
+                    out=sine[:].rearrange(flat_tb), in_=tiles["angle", c][:].rearrange(flat_tb),
+                    func=ACT.Sin, scale=TURN,
+                )
+                tiles["sine", c] = sine
+
+        def scale_and_group(c):
+            if exists(c):
+                z_grouped = stage.tile([P, CHUNK, PACK], BF16, align_bytes=64)
+                nc.vector.tensor_tensor(
+                    out=z_grouped[:],
+                    in0=tiles["sine", c][:].rearrange("p t b -> p b t"),
+                    in1=amplitude[:].unsqueeze(1).to_broadcast([P, CHUNK, PACK]),
+                    op=ALU.mult,
+                )
+                tiles["z_grouped", c] = z_grouped
+
+        def quantise_z(c):
+            if exists(c):
+                z_codes = stage.tile([P, CHUNK], U32, align_bytes=64)
+                z_scales = stage.tile([P, CHUNK], U8, align_bytes=64)
+                nc.vector.quantize_mx(
+                    out=z_codes[:].bitcast(FP8X4),
+                    scales=z_scales[:],
+                    in_=tiles["z_grouped", c][:].rearrange("p b t -> p (b t)"),
+                )
+                tiles["z", c] = (z_codes, z_scales)
+
+        def second_product(c, i):
+            if exists(c):
+                z_codes, z_scales = tiles["z", c]
                 rows = slice(i * P, (i + 1) * P)
-                result = results.tile([P, N_OUT], F32)
+                banks = []
                 for n in range(N_OUT // N_BANK):
                     cols = slice(n * N_BANK, (n + 1) * N_BANK)
                     acc = psum_out.tile([P, N_BANK], F32)
@@ -323,20 +369,56 @@ def tile_unifiedautoencodernet_pa_kernel(tc, h_enc2, We3, be3, P_angles, Wd1, bd
                         start=True,
                         stop=True,
                     )
+                    banks.append(acc)
+                tiles["acc", c, i] = banks
+
+        def add_bias(c, i):
+            if exists(c):
+                result = results.tile([P, N_OUT], F32)
+                for n, acc in enumerate(tiles["acc", c, i]):
+                    cols = slice(n * N_BANK, (n + 1) * N_BANK)
                     nc.vector.tensor_tensor(out=result[:, cols], in0=acc[:], in1=bias[:, cols], op=ALU.add)
+                tiles["result", c, i] = result
+
+        def relu_and_store(c, i):
+            if exists(c):
+                result = tiles["result", c, i]
                 nc.scalar.activation(out=result[:], in_=result[:], func=ACT.Relu)
+                rows_out = out[c * CHUNK : (c + 1) * CHUNK, :].rearrange("(p i) n -> p i n", i=ROW_TILES)
                 nc.sync.dma_start(out=rows_out[:, i, :], in_=result[:])
 
-        quantise_chunk(0)
+        def prepare_chunk(c):
+            transpose_chunk(c)
+            regroup_chunk(c)
+            quantise_chunk(c)
+
+        prepare_chunk(0)
         for t in range(Q_TILES):
-            quantise_along_k1([w1_raw[:, t, :]], w1_codes[:, t], w1_scales[:, t])
-        th_banks = first_product(0)
+            quantise_rows(regroup_rows(transpose_rows([w1_raw[:, t, :]])), w1_codes[:, t], w1_scales[:, t])
+        first_product(0)
         quantise_w2()
-        quantise_chunk(1)
-        for c in range(N_CHUNKS):
-            z_codes, z_scales = circuit(th_banks)
-            if c + 1 < N_CHUNKS:
-                th_banks = first_product(c + 1)
-            if c + 2 < N_CHUNKS:
-                quantise_chunk(c + 2)
-            second_product(c, z_codes, z_scales)
+        for c in range(1, HEAD_CHUNKS):
+            prepare_chunk(c)
+
+        with tc.manual_schedule():
+            for s in range(-2, N_CHUNKS + 1):
+                if s + 4 >= HEAD_CHUNKS:
+                    regroup_chunk(s + 4)
+                add_bias(s - 1, 0)
+                scale_and_group(s)
+                if s + 2 > 0:
+                    first_product(s + 2)
+                angle_in_turns(s + 2)
+                fraction_of_turn(s + 1)
+                sine_of_angle(s + 1)
+                relu_and_store(s - 1, 0)
+                quantise_z(s)
+                add_bias(s - 1, 1)
+                second_product(s, 0)
+                if s + 4 >= HEAD_CHUNKS:
+                    quantise_chunk(s + 4)
+                nearest_turn(s + 2)
+                if s + 5 >= HEAD_CHUNKS:
+                    transpose_chunk(s + 5)
+                relu_and_store(s - 1, 1)
+                second_product(s, 1)

@@ -34,7 +34,7 @@ FLOPS = 2 * BATCH * K1 * QUBITS + 2 * BATCH * QUBITS * N_OUT
 TURN = 2.0 * math.pi
 ROUNDER = 12582912.0
 TINY = 1e-30
-PHASE_STEPS = 3
+RUN = 4
 HEAD_CHUNKS = 3
 
 
@@ -48,6 +48,7 @@ def tile_unifiedautoencodernet_pa_kernel(tc, h_enc2, We3, be3, P_angles, Wd1, bd
         psum_turned = ctx.enter_context(tc.psum_pool(name="psum_turned", bufs=2))
         psum_th = ctx.enter_context(tc.psum_pool(name="psum_th", bufs=2))
         psum_out = ctx.enter_context(tc.psum_pool(name="psum_out", bufs=4))
+        ctx.enter_context(tc.manual_schedule())
 
         angles_bf = small.tile([P, 2, PACK, 3], BF16)
         nc.scalar.dma_start(out=angles_bf[:], in_=P_angles.rearrange("l (p t) a -> p l t a", t=PACK))
@@ -65,9 +66,10 @@ def tile_unifiedautoencodernet_pa_kernel(tc, h_enc2, We3, be3, P_angles, Wd1, bd
 
         load_chunk(0)
         nc.sync.dma_start(out=w1_raw[:], in_=We3.rearrange("(p t) k -> p t k", t=Q_TILES))
-        load_chunk(1)
+        for c in range(1, HEAD_CHUNKS):
+            load_chunk(c)
         nc.sync.dma_start(out=w2_raw[:], in_=Wd1.rearrange("(i p) q -> p i q", p=P))
-        for c in range(2, N_CHUNKS):
+        for c in range(HEAD_CHUNKS, N_CHUNKS):
             load_chunk(c)
         nc.sync.dma_start(out=bias[:], in_=bd1.partition_broadcast(P))
 
@@ -78,127 +80,6 @@ def tile_unifiedautoencodernet_pa_kernel(tc, h_enc2, We3, be3, P_angles, Wd1, bd
         warm = small.tile([P, 1], F32)
         nc.vector.memset(warm[:], 0.0)
         nc.scalar.activation(out=warm[:], in_=warm[:], func=ACT.Sin)
-
-        def product(dst, a, b):
-            nc.vector.tensor_tensor(out=dst, in0=a, in1=b, op=ALU.mult)
-
-        def both(x):
-            return x.unsqueeze(1).to_broadcast([P, 2, PACK])
-
-        turns = small.tile([P, 2, 2, PACK, 3], F32)
-        nc.vector.tensor_scalar(
-            out=turns[:, 0], in0=angles_bf[:], scalar1=1.0 / TURN, scalar2=None, op0=ALU.mult
-        )
-        nc.vector.tensor_scalar(
-            out=turns[:, 1], in0=angles_bf[:], scalar1=1.0 / TURN, scalar2=0.25,
-            op0=ALU.mult, op1=ALU.add,
-        )
-        flat = "p f l t a -> p (f l t a)"
-        whole = small.tile([P, 2, 2, PACK, 3], F32)
-        nc.vector.tensor_scalar(
-            out=whole[:].rearrange(flat), in0=turns[:].rearrange(flat),
-            scalar1=ROUNDER, scalar2=ROUNDER, op0=ALU.add, op1=ALU.subtract,
-        )
-        nc.vector.tensor_tensor(
-            out=turns[:].rearrange(flat), in0=turns[:].rearrange(flat),
-            in1=whole[:].rearrange(flat), op=ALU.subtract,
-        )
-        trig = small.tile([P, 2, 2, PACK, 3], F32)
-        nc.scalar.activation(
-            out=trig[:].rearrange(flat), in_=turns[:].rearrange(flat), func=ACT.Sin, scale=TURN
-        )
-
-        def sin_of(layer, gate):
-            return trig[:, 0, layer, :, gate]
-
-        def cos_of(layer, gate):
-            return trig[:, 1, layer, :, gate]
-
-        def sin_cos_of(layer, gate):
-            return trig[:, :, layer, :, gate]
-
-        RX, RY, RZ = 0, 1, 2
-        SIN, COS = 0, 1
-        yz = small.tile([P, 2, PACK], F32)
-        product(yz[:], both(cos_of(1, RY)), sin_cos_of(1, RX))
-        x_parts = small.tile([P, 2, PACK], F32)
-        product(x_parts[:], both(sin_of(1, RY)), sin_cos_of(0, RZ))
-        y_parts = small.tile([P, 2, PACK], F32)
-        product(y_parts[:], both(yz[:, 0, :]), sin_cos_of(0, RZ))
-        wx = small.tile([P, PACK], F32)
-        nc.vector.tensor_tensor(out=wx[:], in0=y_parts[:, SIN, :], in1=x_parts[:, COS, :], op=ALU.subtract)
-        wy = small.tile([P, PACK], F32)
-        nc.vector.tensor_tensor(out=wy[:], in0=x_parts[:, SIN, :], in1=y_parts[:, COS, :], op=ALU.add)
-        z_parts = small.tile([P, 2, PACK], F32)
-        product(z_parts[:], both(yz[:, 1, :]), sin_cos_of(0, RY))
-        x_parts2 = small.tile([P, 2, PACK], F32)
-        product(x_parts2[:], both(wx[:]), sin_cos_of(0, RY))
-        a_c = small.tile([P, 2, PACK], F32)
-        nc.vector.tensor_tensor(
-            out=a_c[:, 0, :], in0=x_parts2[:, COS, :], in1=z_parts[:, SIN, :], op=ALU.subtract
-        )
-        wz = small.tile([P, PACK], F32)
-        nc.vector.tensor_tensor(out=wz[:], in0=x_parts2[:, SIN, :], in1=z_parts[:, COS, :], op=ALU.add)
-        wy_sin = small.tile([P, PACK], F32)
-        product(wy_sin[:], wy[:], sin_of(0, RX))
-        wz_cos = small.tile([P, PACK], F32)
-        product(wz_cos[:], wz[:], cos_of(0, RX))
-        nc.vector.tensor_tensor(out=a_c[:, 1, :], in0=wz_cos[:], in1=wy_sin[:], op=ALU.subtract)
-
-        squares = small.tile([P, 2, PACK], F32)
-        product(squares[:], a_c[:], a_c[:])
-        length2 = small.tile([P, PACK], F32)
-        nc.vector.scalar_tensor_tensor(
-            out=length2[:], in0=squares[:, 0, :], scalar=TINY, in1=squares[:, 1, :],
-            op0=ALU.add, op1=ALU.add,
-        )
-        inv_length = small.tile([P, PACK], F32)
-        nc.gpsimd.tensor_tensor(out=inv_length[:], in0=length2[:], in1=minus_half[:], op=ALU.pow)
-        twice_positive = small.tile([P, PACK], F32)
-        nc.vector.tensor_scalar(
-            out=twice_positive[:], in0=a_c[:, 0, :], scalar1=0.0, scalar2=2.0,
-            op0=ALU.is_ge, op1=ALU.mult,
-        )
-        inv_m = small.tile([P, PACK], F32)
-        nc.vector.scalar_tensor_tensor(
-            out=inv_m[:], in0=twice_positive[:], scalar=1.0, in1=inv_length[:],
-            op0=ALU.subtract, op1=ALU.mult,
-        )
-        amplitude = small.tile([P, PACK], F32)
-        product(amplitude[:], length2[:], inv_m[:])
-        unit = small.tile([P, 2, PACK], F32)
-        product(unit[:], a_c[:], both(inv_m[:]))
-        cos_goal = unit[:, 0, :]
-        sin_goal = unit[:, 1, :]
-
-        phase = small.tile([P, PACK], F32)
-        nc.vector.tensor_copy(out=phase[:], in_=sin_goal)
-        for step in range(PHASE_STEPS):
-            sin_x = small.tile([P, PACK], F32)
-            nc.scalar.activation(out=sin_x[:], in_=phase[:], func=ACT.Sin)
-            sin_half = small.tile([P, PACK], F32)
-            nc.scalar.activation(out=sin_half[:], in_=phase[:], func=ACT.Sin, scale=0.5)
-            base = small.tile([P, PACK], F32)
-            nc.vector.tensor_tensor(out=base[:], in0=phase[:], in1=sin_goal, op=ALU.add)
-            drop = small.tile([P, PACK], F32)
-            product(drop[:], cos_goal, sin_x[:])
-            half2 = small.tile([P, PACK], F32)
-            product(half2[:], sin_half[:], sin_half[:])
-            nc.vector.tensor_tensor(out=base[:], in0=base[:], in1=drop[:], op=ALU.subtract)
-            nc.vector.scalar_tensor_tensor(
-                out=half2[:], in0=half2[:], scalar=2.0, in1=sin_goal, op0=ALU.mult, op1=ALU.mult
-            )
-            nc.vector.tensor_tensor(out=phase[:], in0=base[:], in1=half2[:], op=ALU.subtract)
-
-        be3_turns = small.tile([P, PACK], F32)
-        nc.vector.tensor_scalar(
-            out=be3_turns[:], in0=be3_bf[:], scalar1=1.0 / TURN, scalar2=None, op0=ALU.mult
-        )
-        shift = small.tile([P, PACK], F32)
-        nc.vector.scalar_tensor_tensor(
-            out=shift[:], in0=phase[:], scalar=1.0 / TURN, in1=be3_turns[:],
-            op0=ALU.mult, op1=ALU.add,
-        )
 
         h_codes = keep.tile([P, N_CHUNKS, PASSES1, CHUNK], U32, align_bytes=64)
         h_scales = keep.tile([P, N_CHUNKS, PASSES1, CHUNK], U8, align_bytes=64)
@@ -237,24 +118,26 @@ def tile_unifiedautoencodernet_pa_kernel(tc, h_enc2, We3, be3, P_angles, Wd1, bd
         w2_codes = keep.tile([P, N_OUT], U32, align_bytes=64)
         w2_scales = keep.tile([P, N_OUT], U8, align_bytes=64)
 
-        def quantise_w2():
+        def prepare_w2(pair):
             words = w2_raw[:].bitcast(F32).rearrange("p i (w u) -> p i u w", u=PAIRS)
-            for pair in range(N_OUT // (2 * P)):
-                grouped2 = stage.tile([P, 2 * P, PACK], BF16, align_bytes=64)
-                turned = psum_turned.tile([P, 2, PAIRS, P], F32)
-                for i in range(2):
-                    for u in range(PAIRS):
-                        nc.tensor.transpose(turned[:, i, u, :], words[:, 2 * pair + i, u, :], identity[:])
-                nc.scalar.copy(
-                    out=grouped2[:].bitcast(F32).rearrange("p (i r) u -> p i r u", i=2),
-                    in_=turned[:].rearrange("p i u r -> p i r u"),
-                )
-                cols = slice(pair * 2 * P, (pair + 1) * 2 * P)
-                nc.vector.quantize_mx(
-                    out=w2_codes[:, cols].bitcast(FP8X4),
-                    scales=w2_scales[:, cols],
-                    in_=grouped2[:].rearrange("p r j -> p (r j)"),
-                )
+            grouped2 = stage.tile([P, 2 * P, PACK], BF16, align_bytes=64)
+            turned = psum_turned.tile([P, 2, PAIRS, P], F32)
+            for i in range(2):
+                for u in range(PAIRS):
+                    nc.tensor.transpose(turned[:, i, u, :], words[:, 2 * pair + i, u, :], identity[:])
+            nc.scalar.copy(
+                out=grouped2[:].bitcast(F32).rearrange("p (i r) u -> p i r u", i=2),
+                in_=turned[:].rearrange("p i u r -> p i r u"),
+            )
+            cols = slice(pair * 2 * P, (pair + 1) * 2 * P)
+            nc.vector.quantize_mx(
+                out=w2_codes[:, cols].bitcast(FP8X4),
+                scales=w2_scales[:, cols],
+                in_=grouped2[:].rearrange("p r j -> p (r j)"),
+            )
+
+        def prepare_w1(t):
+            quantise_rows(regroup_rows(transpose_rows([w1_raw[:, t, :]])), w1_codes[:, t], w1_scales[:, t])
 
         tiles = {}
         flat_tb = "p t b -> p (t b)"
@@ -334,9 +217,9 @@ def tile_unifiedautoencodernet_pa_kernel(tc, h_enc2, We3, be3, P_angles, Wd1, bd
             if exists(c):
                 z_grouped = stage.tile([P, CHUNK, PACK], BF16, align_bytes=64)
                 nc.vector.tensor_tensor(
-                    out=z_grouped[:],
-                    in0=tiles["sine", c][:].rearrange("p t b -> p b t"),
-                    in1=amplitude[:].unsqueeze(1).to_broadcast([P, CHUNK, PACK]),
+                    out=z_grouped[:].rearrange("p (c i) t -> p c t i", i=RUN),
+                    in0=tiles["sine", c][:].rearrange("p t (c i) -> p c t i", i=RUN),
+                    in1=amplitude[:].unsqueeze(1).unsqueeze(3).to_broadcast([P, CHUNK // RUN, PACK, RUN]),
                     op=ALU.mult,
                 )
                 tiles["z_grouped", c] = z_grouped
@@ -392,33 +275,193 @@ def tile_unifiedautoencodernet_pa_kernel(tc, h_enc2, We3, be3, P_angles, Wd1, bd
             regroup_chunk(c)
             quantise_chunk(c)
 
-        prepare_chunk(0)
-        for t in range(Q_TILES):
-            quantise_rows(regroup_rows(transpose_rows([w1_raw[:, t, :]])), w1_codes[:, t], w1_scales[:, t])
-        first_product(0)
-        quantise_w2()
-        for c in range(1, HEAD_CHUNKS):
-            prepare_chunk(c)
+        def product(dst, a, b):
+            nc.vector.tensor_tensor(out=dst, in0=a, in1=b, op=ALU.mult)
 
-        with tc.manual_schedule():
-            for s in range(-2, N_CHUNKS + 1):
-                if s + 4 >= HEAD_CHUNKS:
-                    regroup_chunk(s + 4)
-                add_bias(s - 1, 0)
-                scale_and_group(s)
-                if s + 2 > 0:
-                    first_product(s + 2)
-                angle_in_turns(s + 2)
-                fraction_of_turn(s + 1)
-                sine_of_angle(s + 1)
-                relu_and_store(s - 1, 0)
-                quantise_z(s)
-                add_bias(s - 1, 1)
-                second_product(s, 0)
-                if s + 4 >= HEAD_CHUNKS:
-                    quantise_chunk(s + 4)
-                nearest_turn(s + 2)
-                if s + 5 >= HEAD_CHUNKS:
-                    transpose_chunk(s + 5)
-                relu_and_store(s - 1, 1)
-                second_product(s, 1)
+        def minus_product(dst, a, b):
+            nc.vector.scalar_tensor_tensor(out=dst, in0=a, scalar=-1.0, in1=b, op0=ALU.mult, op1=ALU.mult)
+
+        def both(x):
+            return x.unsqueeze(1).to_broadcast([P, 2, PACK])
+
+        turns = small.tile([P, 2, 2, PACK, 3], F32)
+        nc.vector.tensor_scalar(
+            out=turns[:, 0], in0=angles_bf[:], scalar1=1.0 / TURN, scalar2=None, op0=ALU.mult
+        )
+        nc.vector.tensor_scalar(
+            out=turns[:, 1], in0=angles_bf[:], scalar1=1.0 / TURN, scalar2=0.25,
+            op0=ALU.mult, op1=ALU.add,
+        )
+        flat = "p f l t a -> p (f l t a)"
+        whole = small.tile([P, 2, 2, PACK, 3], F32)
+        nc.vector.tensor_scalar(
+            out=whole[:].rearrange(flat), in0=turns[:].rearrange(flat),
+            scalar1=ROUNDER, scalar2=ROUNDER, op0=ALU.add, op1=ALU.subtract,
+        )
+        nc.vector.tensor_tensor(
+            out=turns[:].rearrange(flat), in0=turns[:].rearrange(flat),
+            in1=whole[:].rearrange(flat), op=ALU.subtract,
+        )
+        trig = small.tile([P, 2, 2, PACK, 3], F32)
+        nc.scalar.activation(
+            out=trig[:].rearrange(flat), in_=turns[:].rearrange(flat), func=ACT.Sin, scale=TURN
+        )
+        be3_turns = small.tile([P, PACK], F32)
+        nc.vector.tensor_scalar(
+            out=be3_turns[:], in0=be3_bf[:], scalar1=1.0 / TURN, scalar2=None, op0=ALU.mult
+        )
+
+        def sin_of(layer, gate):
+            return trig[:, 0, layer, :, gate]
+
+        def cos_of(layer, gate):
+            return trig[:, 1, layer, :, gate]
+
+        def sin_cos_of(layer, gate):
+            return trig[:, :, layer, :, gate]
+
+        RX, RY, RZ = 0, 1, 2
+        layer1 = small.tile([P, 2, PACK], F32)
+        product(layer1[:], both(cos_of(1, RY)), sin_cos_of(1, RX))
+        cx0_y0 = small.tile([P, 2, PACK], F32)
+        product(cx0_y0[:], both(cos_of(0, RX)), sin_cos_of(0, RY))
+        cy0_z0 = small.tile([P, 2, PACK], F32)
+        product(cy0_z0[:], both(cos_of(0, RY)), sin_cos_of(0, RZ))
+        sx0_z0 = small.tile([P, 2, PACK], F32)
+        product(sx0_z0[:], both(sin_of(0, RX)), sin_cos_of(0, RZ))
+        cx0_sy0_z0 = small.tile([P, 2, PACK], F32)
+        product(cx0_sy0_z0[:], both(cx0_y0[:, 0, :]), sin_cos_of(0, RZ))
+        cy1_sx1 = layer1[:, 0, :]
+        cy1_cx1 = layer1[:, 1, :]
+        sy1 = sin_of(1, RY)
+        A_TERMS = 3
+        terms = small.tile([P, 8, PACK], F32)
+        product(terms[:, 0, :], cy0_z0[:, 0, :], cy1_sx1)
+        minus_product(terms[:, 1, :], cy0_z0[:, 1, :], sy1)
+        minus_product(terms[:, 2, :], sin_of(0, RY), cy1_cx1)
+        minus_product(terms[:, 3, :], sx0_z0[:, 0, :], sy1)
+        minus_product(terms[:, 4, :], sx0_z0[:, 1, :], cy1_sx1)
+        product(terms[:, 5, :], cx0_y0[:, 1, :], cy1_cx1)
+        product(terms[:, 6, :], cx0_sy0_z0[:, 0, :], cy1_sx1)
+        minus_product(terms[:, 7, :], cx0_sy0_z0[:, 1, :], sy1)
+        a_c = small.tile([P, 2, PACK], F32)
+        nc.vector.tensor_reduce(
+            out=a_c[:, 0, :], in_=terms[:, :A_TERMS, :].rearrange("p j t -> p t j"),
+            axis=mybir.AxisListType.X, op=ALU.add,
+        )
+        nc.vector.tensor_reduce(
+            out=a_c[:, 1, :], in_=terms[:, A_TERMS:, :].rearrange("p j t -> p t j"),
+            axis=mybir.AxisListType.X, op=ALU.add,
+        )
+
+        prepare_chunk(0)
+
+        twice_positive = small.tile([P, PACK], F32)
+        nc.vector.tensor_scalar(
+            out=twice_positive[:], in0=a_c[:, 0, :], scalar1=0.0, scalar2=2.0,
+            op0=ALU.is_ge, op1=ALU.mult,
+        )
+        squares = small.tile([P, 2, PACK], F32)
+        product(squares[:], a_c[:], a_c[:])
+        absolute = small.tile([P, 2, PACK], F32)
+        nc.vector.scalar_tensor_tensor(
+            out=absolute[:], in0=a_c[:], scalar=-1.0, in1=a_c[:], op0=ALU.mult, op1=ALU.max
+        )
+        length2 = small.tile([P, PACK], F32)
+        nc.vector.scalar_tensor_tensor(
+            out=length2[:], in0=squares[:, 0, :], scalar=TINY, in1=squares[:, 1, :],
+            op0=ALU.add, op1=ALU.add,
+        )
+        inv_length = small.tile([P, PACK], F32)
+        nc.gpsimd.tensor_tensor(out=inv_length[:], in0=length2[:], in1=minus_half[:], op=ALU.pow)
+
+        girth = small.tile([P, PACK], F32)
+        nc.vector.scalar_tensor_tensor(
+            out=girth[:], in0=absolute[:, 0, :], scalar=TINY, in1=absolute[:, 1, :],
+            op0=ALU.add, op1=ALU.add,
+        )
+        c_signed = small.tile([P, PACK], F32)
+        nc.vector.scalar_tensor_tensor(
+            out=c_signed[:], in0=twice_positive[:], scalar=1.0, in1=a_c[:, 1, :],
+            op0=ALU.subtract, op1=ALU.mult,
+        )
+        inv_girth = small.tile([P, PACK], F32)
+        nc.vector.reciprocal(out=inv_girth[:], in_=girth[:])
+        phase = small.tile([P, PACK], F32)
+        nc.vector.scalar_tensor_tensor(
+            out=phase[:], in0=c_signed[:], scalar=0.25 * TURN, in1=inv_girth[:],
+            op0=ALU.mult, op1=ALU.mult,
+        )
+        for t in range(Q_TILES):
+            prepare_w1(t)
+        inv_m = small.tile([P, PACK], F32)
+        nc.vector.scalar_tensor_tensor(
+            out=inv_m[:], in0=twice_positive[:], scalar=1.0, in1=inv_length[:],
+            op0=ALU.subtract, op1=ALU.mult,
+        )
+        unit = small.tile([P, 2, PACK], F32)
+        product(unit[:], a_c[:], both(inv_m[:]))
+        cos_goal = unit[:, 0, :]
+        sin_goal = unit[:, 1, :]
+        amplitude = small.tile([P, PACK], F32)
+        product(amplitude[:], length2[:], inv_m[:])
+        first_product(0)
+
+        def sines_of_phase():
+            sin_x = small.tile([P, PACK], F32)
+            nc.scalar.activation(out=sin_x[:], in_=phase[:], func=ACT.Sin)
+            sin_half = small.tile([P, PACK], F32)
+            nc.scalar.activation(out=sin_half[:], in_=phase[:], func=ACT.Sin, scale=0.5)
+            return sin_x, sin_half
+
+        def improve_phase(sin_x, sin_half):
+            base = small.tile([P, PACK], F32)
+            nc.vector.tensor_tensor(out=base[:], in0=phase[:], in1=sin_goal, op=ALU.add)
+            drop = small.tile([P, PACK], F32)
+            product(drop[:], cos_goal, sin_x[:])
+            half2 = small.tile([P, PACK], F32)
+            product(half2[:], sin_half[:], sin_half[:])
+            nc.vector.tensor_tensor(out=base[:], in0=base[:], in1=drop[:], op=ALU.subtract)
+            nc.vector.scalar_tensor_tensor(
+                out=half2[:], in0=half2[:], scalar=2.0, in1=sin_goal, op0=ALU.mult, op1=ALU.mult
+            )
+            nc.vector.tensor_tensor(out=phase[:], in0=base[:], in1=half2[:], op=ALU.subtract)
+
+        sin_x, sin_half = sines_of_phase()
+        prepare_chunk(1)
+        improve_phase(sin_x, sin_half)
+        prepare_chunk(2)
+        sin_x, sin_half = sines_of_phase()
+        prepare_w2(0)
+        improve_phase(sin_x, sin_half)
+        prepare_w2(1)
+
+        shift = small.tile([P, PACK], F32)
+        nc.vector.scalar_tensor_tensor(
+            out=shift[:], in0=phase[:], scalar=1.0 / TURN, in1=be3_turns[:],
+            op0=ALU.mult, op1=ALU.add,
+        )
+
+        prepare_w2(2)
+        prepare_w2(3)
+
+        for s in range(-2, N_CHUNKS + 1):
+            if s + 4 >= HEAD_CHUNKS:
+                regroup_chunk(s + 4)
+            add_bias(s - 1, 0)
+            scale_and_group(s)
+            angle_in_turns(s + 2)
+            fraction_of_turn(s + 1)
+            sine_of_angle(s + 1)
+            relu_and_store(s - 1, 0)
+            quantise_z(s)
+            add_bias(s - 1, 1)
+            second_product(s, 0)
+            if s + 4 >= HEAD_CHUNKS:
+                quantise_chunk(s + 4)
+            nearest_turn(s + 2)
+            if s + 5 >= HEAD_CHUNKS:
+                transpose_chunk(s + 5)
+            relu_and_store(s - 1, 1)
+            second_product(s, 1)
+            first_product(s + 3)

@@ -266,9 +266,11 @@ def tile_unifiedautoencodernet_pa_kernel(tc, h_enc2, We3, be3, P_angles, Wd1, bd
         def relu_and_store(c, i):
             if exists(c):
                 result = tiles["result", c, i]
-                nc.scalar.activation(out=result[:], in_=result[:], func=ACT.Relu)
                 rows_out = out[c * CHUNK : (c + 1) * CHUNK, :].rearrange("(p i) n -> p i n", i=ROW_TILES)
-                nc.sync.dma_start(out=rows_out[:, i, :], in_=result[:])
+                for n in range(N_OUT // N_BANK):
+                    cols = slice(n * N_BANK, (n + 1) * N_BANK)
+                    nc.scalar.activation(out=result[:, cols], in_=result[:, cols], func=ACT.Relu)
+                    nc.sync.dma_start(out=rows_out[:, i, cols], in_=result[:, cols])
 
         def prepare_chunk(c):
             transpose_chunk(c)
@@ -405,7 +407,6 @@ def tile_unifiedautoencodernet_pa_kernel(tc, h_enc2, We3, be3, P_angles, Wd1, bd
         sin_goal = unit[:, 1, :]
         amplitude = small.tile([P, PACK], F32)
         product(amplitude[:], length2[:], inv_m[:])
-        first_product(0)
 
         def sines_of_phase():
             sin_x = small.tile([P, PACK], F32)
@@ -428,8 +429,11 @@ def tile_unifiedautoencodernet_pa_kernel(tc, h_enc2, We3, be3, P_angles, Wd1, bd
             nc.vector.tensor_tensor(out=phase[:], in0=base[:], in1=half2[:], op=ALU.subtract)
 
         sin_x, sin_half = sines_of_phase()
-        prepare_chunk(1)
+        transpose_chunk(1)
         improve_phase(sin_x, sin_half)
+        regroup_chunk(1)
+        quantise_chunk(1)
+        first_product(0)
         prepare_chunk(2)
         sin_x, sin_half = sines_of_phase()
         prepare_w2(0)

@@ -45,9 +45,8 @@ def tile_unifiedautoencodernet_pa_kernel(tc, h_enc2, We3, be3, P_angles, Wd1, bd
         small = ctx.enter_context(tc.tile_pool(name="small", bufs=1))
         stage = ctx.enter_context(tc.tile_pool(name="stage", bufs=3))
         results = ctx.enter_context(tc.tile_pool(name="results", bufs=6))
-        psum_turned = ctx.enter_context(tc.psum_pool(name="psum_turned", bufs=2))
         psum_th = ctx.enter_context(tc.psum_pool(name="psum_th", bufs=2))
-        psum_out = ctx.enter_context(tc.psum_pool(name="psum_out", bufs=4))
+        psum_work = ctx.enter_context(tc.psum_pool(name="psum_work", bufs=6))
         ctx.enter_context(tc.manual_schedule())
 
         angles_bf = small.tile([P, 2, PACK, 3], BF16)
@@ -90,7 +89,7 @@ def tile_unifiedautoencodernet_pa_kernel(tc, h_enc2, We3, be3, P_angles, Wd1, bd
             banks = []
             for rows in row_tiles:
                 words = rows.bitcast(F32)
-                turned = psum_turned.tile([P, PASSES1, PAIRS, P], F32)
+                turned = psum_work.tile([P, PASSES1, PAIRS, P], F32, tag="bank")
                 for g in range(PASSES1):
                     for u in range(PAIRS):
                         first = (g * PAIRS + u) * P
@@ -121,7 +120,7 @@ def tile_unifiedautoencodernet_pa_kernel(tc, h_enc2, We3, be3, P_angles, Wd1, bd
         def prepare_w2(pair):
             words = w2_raw[:].bitcast(F32).rearrange("p i (w u) -> p i u w", u=PAIRS)
             grouped2 = stage.tile([P, 2 * P, PACK], BF16, align_bytes=64)
-            turned = psum_turned.tile([P, 2, PAIRS, P], F32)
+            turned = psum_work.tile([P, 2, PAIRS, P], F32, tag="bank")
             for i in range(2):
                 for u in range(PAIRS):
                     nc.tensor.transpose(turned[:, i, u, :], words[:, 2 * pair + i, u, :], identity[:])
@@ -242,7 +241,7 @@ def tile_unifiedautoencodernet_pa_kernel(tc, h_enc2, We3, be3, P_angles, Wd1, bd
                 banks = []
                 for n in range(N_OUT // N_BANK):
                     cols = slice(n * N_BANK, (n + 1) * N_BANK)
-                    acc = psum_out.tile([P, N_BANK], F32)
+                    acc = psum_work.tile([P, N_BANK], F32, tag="bank")
                     nc.tensor.matmul_mx(
                         out=acc[:],
                         lhsT=z_codes[:, rows].bitcast(FP8X4),

import math
from contextlib import ExitStack

import concourse.mybir as mybir
from concourse.masks import make_identity

F32 = mybir.dt.float32
BF16 = mybir.dt.bfloat16
U32 = mybir.dt.uint32
U8 = mybir.dt.uint8
FP8X4 = mybir.dt.float8_e4m3fn_x4
ALU = mybir.AluOpType
ACT = mybir.ActivationFunctionType

P = 128
PACK = 4
K_PASS = P * PACK

BATCH = 2048
K1 = 1024
QUBITS = 512
N_OUT = 1024
PASSES1 = K1 // K_PASS
PAIRS = 2
Q_TILES = QUBITS // P
N_BANK = 512

ROW_TILES = 2
CHUNK = ROW_TILES * P
N_CHUNKS = BATCH // CHUNK

FLOPS = 2 * BATCH * K1 * QUBITS + 2 * BATCH * QUBITS * N_OUT

TURN = 2.0 * math.pi
ROUNDER = 12582912.0
TINY = 1e-30
RUN = 4
HEAD_CHUNKS = 3


def tile_unifiedautoencodernet_pa_kernel(tc, h_enc2, We3, be3, P_angles, Wd1, bd1, out):
    nc = tc.nc
    with ExitStack() as ctx:
        keep = ctx.enter_context(tc.tile_pool(name="keep", bufs=1))
        small = ctx.enter_context(tc.tile_pool(name="small", bufs=1))
        stage = ctx.enter_context(tc.tile_pool(name="stage", bufs=3))
        results = ctx.enter_context(tc.tile_pool(name="results", bufs=6))
        psum_th = ctx.enter_context(tc.psum_pool(name="psum_th", bufs=2))
        psum_work = ctx.enter_context(tc.psum_pool(name="psum_work", bufs=6))
        ctx.enter_context(tc.manual_schedule())

        angles_bf = small.tile([P, 2, PACK, 3], BF16)
        nc.scalar.dma_start(out=angles_bf[:], in_=P_angles.rearrange("l (p t) a -> p l t a", t=PACK))
        be3_bf = small.tile([P, PACK], BF16)
        nc.scalar.dma_start(out=be3_bf[:], in_=be3.rearrange("(p t) -> p t", t=PACK))

        h_raw = keep.tile([P, N_CHUNKS, ROW_TILES, K1], BF16)
        w1_raw = keep.tile([P, Q_TILES, K1], BF16)
        w2_raw = keep.tile([P, N_OUT // P, QUBITS], BF16)
        bias = keep.tile([P, N_OUT], BF16)

        def load_chunk(c):
            rows = h_enc2[c * CHUNK : (c + 1) * CHUNK, :]
            nc.sync.dma_start(out=h_raw[:, c], in_=rows.rearrange("(p i) k -> p i k", i=ROW_TILES))

        load_chunk(0)
        nc.sync.dma_start(out=w1_raw[:], in_=We3.rearrange("(p t) k -> p t k", t=Q_TILES))
        for c in range(1, HEAD_CHUNKS):
            load_chunk(c)
        nc.sync.dma_start(out=w2_raw[:], in_=Wd1.rearrange("(i p) q -> p i q", p=P))
        for c in range(HEAD_CHUNKS, N_CHUNKS):
            load_chunk(c)
        nc.sync.dma_start(out=bias[:], in_=bd1.partition_broadcast(P))

        identity = keep.tile([P, P], F32)
        make_identity(nc, identity[:])
        minus_half = small.tile([P, PACK], F32)
        nc.vector.memset(minus_half[:], -0.5)
        warm = small.tile([P, 1], F32)
        nc.vector.memset(warm[:], 0.0)
        nc.scalar.activation(out=warm[:], in_=warm[:], func=ACT.Sin)

        h_codes = keep.tile([P, N_CHUNKS, PASSES1, CHUNK], U32, align_bytes=64)
        h_scales = keep.tile([P, N_CHUNKS, PASSES1, CHUNK], U8, align_bytes=64)
        w1_codes = keep.tile([P, Q_TILES, PASSES1, P], U32, align_bytes=64)
        w1_scales = keep.tile([P, Q_TILES, PASSES1, P], U8, align_bytes=64)

        def transpose_rows(row_tiles):
            banks = []
            for rows in row_tiles:
                words = rows.bitcast(F32)
                turned = psum_work.tile([P, PASSES1, PAIRS, P], F32, tag="bank")
                for g in range(PASSES1):
                    for u in range(PAIRS):
                        first = (g * PAIRS + u) * P
                        nc.tensor.transpose(turned[:, g, u, :], words[:, first : first + P], identity[:])
                banks.append(turned)
            return banks

        def regroup_rows(banks):
            grouped = stage.tile([P, PASSES1, len(banks) * P, PACK], BF16, align_bytes=64)
            grouped_words = grouped[:].bitcast(F32)
            for i, turned in enumerate(banks):
                nc.scalar.copy(
                    out=grouped_words[:, :, i * P : (i + 1) * P, :],
                    in_=turned[:].rearrange("p g u r -> p g r u"),
                )
            return grouped

        def quantise_rows(grouped, codes, scales):
            nc.vector.quantize_mx(
                out=codes.rearrange("p g r -> p (g r)").bitcast(FP8X4),
                scales=scales.rearrange("p g r -> p (g r)"),
                in_=grouped[:].rearrange("p g r j -> p (g r j)"),
            )

        w2_codes = keep.tile([P, N_OUT], U32, align_bytes=64)
        w2_scales = keep.tile([P, N_OUT], U8, align_bytes=64)

        def prepare_w2(pair):
            words = w2_raw[:].bitcast(F32).rearrange("p i (w u) -> p i u w", u=PAIRS)
            grouped2 = stage.tile([P, 2 * P, PACK], BF16, align_bytes=64)
            turned = psum_work.tile([P, 2, PAIRS, P], F32, tag="bank")
            for i in range(2):
                for u in range(PAIRS):
                    nc.tensor.transpose(turned[:, i, u, :], words[:, 2 * pair + i, u, :], identity[:])
            nc.scalar.copy(
                out=grouped2[:].bitcast(F32).rearrange("p (i r) u -> p i r u", i=2),
                in_=turned[:].rearrange("p i u r -> p i r u"),
            )
            cols = slice(pair * 2 * P, (pair + 1) * 2 * P)
            nc.vector.quantize_mx(
                out=w2_codes[:, cols].bitcast(FP8X4),
                scales=w2_scales[:, cols],
                in_=grouped2[:].rearrange("p r j -> p (r j)"),
            )

        def prepare_w1(t):
            quantise_rows(regroup_rows(transpose_rows([w1_raw[:, t, :]])), w1_codes[:, t], w1_scales[:, t])

        tiles = {}
        flat_tb = "p t b -> p (t b)"

        def exists(c):
            return 0 <= c < N_CHUNKS

        def transpose_chunk(c):
            if exists(c):
                tiles["turned", c] = transpose_rows([h_raw[:, c, i, :] for i in range(ROW_TILES)])

        def regroup_chunk(c):
            if exists(c):
                tiles["grouped", c] = regroup_rows(tiles["turned", c])

        def quantise_chunk(c):
            if exists(c):
                quantise_rows(tiles["grouped", c], h_codes[:, c], h_scales[:, c])

        def first_product(c):
            if exists(c):
                banks = []
                for b in range(Q_TILES // 2):
                    th_bank = psum_th.tile([P, 2, CHUNK], F32)
                    for i in range(2):
                        t = 2 * b + i
                        for g in range(PASSES1):
                            nc.tensor.matmul_mx(
                                out=th_bank[:, i, :],
                                lhsT=w1_codes[:, t, g, :].bitcast(FP8X4),
                                lhsT_scale=w1_scales[:, t, g, :],
                                rhs=h_codes[:, c, g, :].bitcast(FP8X4),
                                rhs_scale=h_scales[:, c, g, :],
                                start=(g == 0),
                                stop=(g == PASSES1 - 1),
                            )
                    banks.append(th_bank)
                tiles["th", c] = banks

        def angle_in_turns(c):
            if exists(c):
                angle = stage.tile([P, Q_TILES, CHUNK], F32)
                for t in range(Q_TILES):
                    nc.scalar.activation(
                        out=angle[:, t, :], in_=tiles["th", c][t // 2][:, t % 2, :], func=ACT.Identity,
                        scale=1.0 / TURN, bias=shift[:, t : t + 1],
                    )
                tiles["angle", c] = angle

        def nearest_turn(c):
            if exists(c):
                nearest = stage.tile([P, Q_TILES, CHUNK], F32)
                nc.vector.tensor_scalar(
                    out=nearest[:].rearrange(flat_tb), in0=tiles["angle", c][:].rearrange(flat_tb),
                    scalar1=ROUNDER, scalar2=ROUNDER, op0=ALU.add, op1=ALU.subtract,
                )
                tiles["nearest", c] = nearest

        def fraction_of_turn(c):
            if exists(c):
                angle = tiles["angle", c]
                nc.vector.tensor_tensor(
                    out=angle[:].rearrange(flat_tb), in0=angle[:].rearrange(flat_tb),
                    in1=tiles["nearest", c][:].rearrange(flat_tb), op=ALU.subtract,
                )

        def sine_of_angle(c):
            if exists(c):
                sine = stage.tile([P, Q_TILES, CHUNK], F32)
                nc.scalar.activation(
                    out=sine[:].rearrange(flat_tb), in_=tiles["angle", c][:].rearrange(flat_tb),
                    func=ACT.Sin, scale=TURN,
                )
                tiles["sine", c] = sine

        def scale_and_group(c):
            if exists(c):
                z_grouped = stage.tile([P, CHUNK, PACK], BF16, align_bytes=64)
                nc.vector.tensor_tensor(
                    out=z_grouped[:].rearrange("p (c i) t -> p c t i", i=RUN),
                    in0=tiles["sine", c][:].rearrange("p t (c i) -> p c t i", i=RUN),
                    in1=amplitude[:].unsqueeze(1).unsqueeze(3).to_broadcast([P, CHUNK // RUN, PACK, RUN]),
                    op=ALU.mult,
                )
                tiles["z_grouped", c] = z_grouped

        def quantise_z(c):
            if exists(c):
                z_codes = stage.tile([P, CHUNK], U32, align_bytes=64)
                z_scales = stage.tile([P, CHUNK], U8, align_bytes=64)
                nc.vector.quantize_mx(
                    out=z_codes[:].bitcast(FP8X4),
                    scales=z_scales[:],
                    in_=tiles["z_grouped", c][:].rearrange("p b t -> p (b t)"),
                )
                tiles["z", c] = (z_codes, z_scales)

        def second_product(c, i):
            if exists(c):
                z_codes, z_scales = tiles["z", c]
                rows = slice(i * P, (i + 1) * P)
                banks = []
                for n in range(N_OUT // N_BANK):
                    cols = slice(n * N_BANK, (n + 1) * N_BANK)
                    acc = psum_work.tile([P, N_BANK], F32, tag="bank")
                    nc.tensor.matmul_mx(
                        out=acc[:],
                        lhsT=z_codes[:, rows].bitcast(FP8X4),
                        lhsT_scale=z_scales[:, rows],
                        rhs=w2_codes[:, cols].bitcast(FP8X4),
                        rhs_scale=w2_scales[:, cols],
                        start=True,
                        stop=True,
                    )
                    banks.append(acc)
                tiles["acc", c, i] = banks

        def add_bias(c, i):
            if exists(c):
                result = results.tile([P, N_OUT], F32)
                for n, acc in enumerate(tiles["acc", c, i]):
                    cols = slice(n * N_BANK, (n + 1) * N_BANK)
                    nc.vector.tensor_tensor(out=result[:, cols], in0=acc[:], in1=bias[:, cols], op=ALU.add)
                tiles["result", c, i] = result

        def relu_and_store(c, i):
            if exists(c):
                result = tiles["result", c, i]
                rows_out = out[c * CHUNK : (c + 1) * CHUNK, :].rearrange("(p i) n -> p i n", i=ROW_TILES)
                for n in range(N_OUT // N_BANK):
                    cols = slice(n * N_BANK, (n + 1) * N_BANK)
                    nc.scalar.activation(out=result[:, cols], in_=result[:, cols], func=ACT.Relu)
                    nc.sync.dma_start(out=rows_out[:, i, cols], in_=result[:, cols])

        def prepare_chunk(c):
            transpose_chunk(c)
            regroup_chunk(c)
            quantise_chunk(c)

        def product(dst, a, b):
            nc.vector.tensor_tensor(out=dst, in0=a, in1=b, op=ALU.mult)

        def minus_product(dst, a, b):
            nc.vector.scalar_tensor_tensor(out=dst, in0=a, scalar=-1.0, in1=b, op0=ALU.mult, op1=ALU.mult)

        def both(x):
            return x.unsqueeze(1).to_broadcast([P, 2, PACK])

        turns = small.tile([P, 2, 2, PACK, 3], F32)
        nc.vector.tensor_scalar(
            out=turns[:, 0], in0=angles_bf[:], scalar1=1.0 / TURN, scalar2=None, op0=ALU.mult
        )
        nc.vector.tensor_scalar(
            out=turns[:, 1], in0=angles_bf[:], scalar1=1.0 / TURN, scalar2=0.25,
            op0=ALU.mult, op1=ALU.add,
        )
        flat = "p f l t a -> p (f l t a)"
        whole = small.tile([P, 2, 2, PACK, 3], F32)
        nc.vector.tensor_scalar(
            out=whole[:].rearrange(flat), in0=turns[:].rearrange(flat),
            scalar1=ROUNDER, scalar2=ROUNDER, op0=ALU.add, op1=ALU.subtract,
        )
        nc.vector.tensor_tensor(
            out=turns[:].rearrange(flat), in0=turns[:].rearrange(flat),
            in1=whole[:].rearrange(flat), op=ALU.subtract,
        )
        trig = small.tile([P, 2, 2, PACK, 3], F32)
        nc.scalar.activation(
            out=trig[:].rearrange(flat), in_=turns[:].rearrange(flat), func=ACT.Sin, scale=TURN
        )
        be3_turns = small.tile([P, PACK], F32)
        nc.vector.tensor_scalar(
            out=be3_turns[:], in0=be3_bf[:], scalar1=1.0 / TURN, scalar2=None, op0=ALU.mult
        )

        def sin_of(layer, gate):
            return trig[:, 0, layer, :, gate]

        def cos_of(layer, gate):
            return trig[:, 1, layer, :, gate]

        def sin_cos_of(layer, gate):
            return trig[:, :, layer, :, gate]

        RX, RY, RZ = 0, 1, 2
        layer1 = small.tile([P, 2, PACK], F32)
        product(layer1[:], both(cos_of(1, RY)), sin_cos_of(1, RX))
        cx0_y0 = small.tile([P, 2, PACK], F32)
        product(cx0_y0[:], both(cos_of(0, RX)), sin_cos_of(0, RY))
        cy0_z0 = small.tile([P, 2, PACK], F32)
        product(cy0_z0[:], both(cos_of(0, RY)), sin_cos_of(0, RZ))
        sx0_z0 = small.tile([P, 2, PACK], F32)
        product(sx0_z0[:], both(sin_of(0, RX)), sin_cos_of(0, RZ))
        cx0_sy0_z0 = small.tile([P, 2, PACK], F32)
        product(cx0_sy0_z0[:], both(cx0_y0[:, 0, :]), sin_cos_of(0, RZ))
        cy1_sx1 = layer1[:, 0, :]
        cy1_cx1 = layer1[:, 1, :]
        sy1 = sin_of(1, RY)
        A_TERMS = 3
        terms = small.tile([P, 8, PACK], F32)
        product(terms[:, 0, :], cy0_z0[:, 0, :], cy1_sx1)
        minus_product(terms[:, 1, :], cy0_z0[:, 1, :], sy1)
        minus_product(terms[:, 2, :], sin_of(0, RY), cy1_cx1)
        minus_product(terms[:, 3, :], sx0_z0[:, 0, :], sy1)
        minus_product(terms[:, 4, :], sx0_z0[:, 1, :], cy1_sx1)
        product(terms[:, 5, :], cx0_y0[:, 1, :], cy1_cx1)
        product(terms[:, 6, :], cx0_sy0_z0[:, 0, :], cy1_sx1)
        minus_product(terms[:, 7, :], cx0_sy0_z0[:, 1, :], sy1)
        a_c = small.tile([P, 2, PACK], F32)
        nc.vector.tensor_reduce(
            out=a_c[:, 0, :], in_=terms[:, :A_TERMS, :].rearrange("p j t -> p t j"),
            axis=mybir.AxisListType.X, op=ALU.add,
        )
        nc.vector.tensor_reduce(
            out=a_c[:, 1, :], in_=terms[:, A_TERMS:, :].rearrange("p j t -> p t j"),
            axis=mybir.AxisListType.X, op=ALU.add,
        )

        prepare_chunk(0)

        twice_positive = small.tile([P, PACK], F32)
        nc.vector.tensor_scalar(
            out=twice_positive[:], in0=a_c[:, 0, :], scalar1=0.0, scalar2=2.0,
            op0=ALU.is_ge, op1=ALU.mult,
        )
        squares = small.tile([P, 2, PACK], F32)
        product(squares[:], a_c[:], a_c[:])
        absolute = small.tile([P, 2, PACK], F32)
        nc.vector.scalar_tensor_tensor(
            out=absolute[:], in0=a_c[:], scalar=-1.0, in1=a_c[:], op0=ALU.mult, op1=ALU.max
        )
        length2 = small.tile([P, PACK], F32)
        nc.vector.scalar_tensor_tensor(
            out=length2[:], in0=squares[:, 0, :], scalar=TINY, in1=squares[:, 1, :],
            op0=ALU.add, op1=ALU.add,
        )
        inv_length = small.tile([P, PACK], F32)
        nc.gpsimd.tensor_tensor(out=inv_length[:], in0=length2[:], in1=minus_half[:], op=ALU.pow)

        girth = small.tile([P, PACK], F32)
        nc.vector.scalar_tensor_tensor(
            out=girth[:], in0=absolute[:, 0, :], scalar=TINY, in1=absolute[:, 1, :],
            op0=ALU.add, op1=ALU.add,
        )
        c_signed = small.tile([P, PACK], F32)
        nc.vector.scalar_tensor_tensor(
            out=c_signed[:], in0=twice_positive[:], scalar=1.0, in1=a_c[:, 1, :],
            op0=ALU.subtract, op1=ALU.mult,
        )
        inv_girth = small.tile([P, PACK], F32)
        nc.vector.reciprocal(out=inv_girth[:], in_=girth[:])
        phase = small.tile([P, PACK], F32)
        nc.vector.scalar_tensor_tensor(
            out=phase[:], in0=c_signed[:], scalar=0.25 * TURN, in1=inv_girth[:],
            op0=ALU.mult, op1=ALU.mult,
        )
        for t in range(Q_TILES):
            prepare_w1(t)
        inv_m = small.tile([P, PACK], F32)
        nc.vector.scalar_tensor_tensor(
            out=inv_m[:], in0=twice_positive[:], scalar=1.0, in1=inv_length[:],
            op0=ALU.subtract, op1=ALU.mult,
        )
        unit = small.tile([P, 2, PACK], F32)
        product(unit[:], a_c[:], both(inv_m[:]))
        cos_goal = unit[:, 0, :]
        sin_goal = unit[:, 1, :]
        amplitude = small.tile([P, PACK], F32)
        product(amplitude[:], length2[:], inv_m[:])

        def sines_of_phase():
            sin_x = small.tile([P, PACK], F32)
            nc.scalar.activation(out=sin_x[:], in_=phase[:], func=ACT.Sin)
            sin_half = small.tile([P, PACK], F32)
            nc.scalar.activation(out=sin_half[:], in_=phase[:], func=ACT.Sin, scale=0.5)
            return sin_x, sin_half

        def improve_phase(sin_x, sin_half):
            base = small.tile([P, PACK], F32)
            nc.vector.tensor_tensor(out=base[:], in0=phase[:], in1=sin_goal, op=ALU.add)
            drop = small.tile([P, PACK], F32)
            product(drop[:], cos_goal, sin_x[:])
            half2 = small.tile([P, PACK], F32)
            product(half2[:], sin_half[:], sin_half[:])
            nc.vector.tensor_tensor(out=base[:], in0=base[:], in1=drop[:], op=ALU.subtract)
            nc.vector.scalar_tensor_tensor(
                out=half2[:], in0=half2[:], scalar=2.0, in1=sin_goal, op0=ALU.mult, op1=ALU.mult
            )
            nc.vector.tensor_tensor(out=phase[:], in0=base[:], in1=half2[:], op=ALU.subtract)

        sin_x, sin_half = sines_of_phase()
        transpose_chunk(1)
        improve_phase(sin_x, sin_half)
        regroup_chunk(1)
        quantise_chunk(1)
        first_product(0)
        prepare_chunk(2)
        sin_x, sin_half = sines_of_phase()
        prepare_w2(0)
        improve_phase(sin_x, sin_half)
        prepare_w2(1)

        shift = small.tile([P, PACK], F32)
        nc.vector.scalar_tensor_tensor(
            out=shift[:], in0=phase[:], scalar=1.0 / TURN, in1=be3_turns[:],
            op0=ALU.mult, op1=ALU.add,
        )

        prepare_w2(2)
        prepare_w2(3)

        for s in range(-2, N_CHUNKS + 1):
            if s + 4 >= HEAD_CHUNKS:
                regroup_chunk(s + 4)
            add_bias(s - 1, 0)
            scale_and_group(s)
            angle_in_turns(s + 2)
            fraction_of_turn(s + 1)
            sine_of_angle(s + 1)
            relu_and_store(s - 1, 0)
            quantise_z(s)
            add_bias(s - 1, 1)
            second_product(s, 0)
            if s + 4 >= HEAD_CHUNKS:
                quantise_chunk(s + 4)
            nearest_turn(s + 2)
            if s + 5 >= HEAD_CHUNKS:
                transpose_chunk(s + 5)
            relu_and_store(s - 1, 1)
            second_product(s, 1)
            first_product(s + 3)
